import numpy as np
import ml_dtypes

BF16 = ml_dtypes.bfloat16


def bf(x):
    return np.asarray(x, np.float32).astype(BF16)


def f32(x):
    return np.asarray(x, np.float32)


def f64(x):
    return np.asarray(x).astype(np.float64)


def striped(idx):
    return np.tile(idx.reshape(-1, 16).T, (8, 1))


C, H, HD, S, N = 256, 2, 128, 512, 256
P_EDGE = 0.03
X_SCALE = 0.4


def setup_inputs():
    base = f32(np.random.standard_normal((C, S)))
    x = f32(X_SCALE * np.random.standard_normal((C, N)))
    adj_t = f32(np.maximum(np.random.random((N, N)) < P_EDGE, np.eye(N)))
    bo = f32(0.1 * np.random.standard_normal((C, 1)))
    return {"base": base, "x": x, "adj_t": adj_t, "bo": bo, "offs": striped(np.random.permutation(S)[:N])}


def reference(base, x, adj_t, bo, offs):
    idx = offs[:16].T.reshape(-1)
    xh = f64(x).reshape(H, HD, N)
    s = np.einsum('hdk,hdj->hkj', xh, xh) / np.sqrt(HD)
    e = np.exp(s) * f64(adj_t)[None]
    a = e / e.sum(axis=1, keepdims=True)
    y = np.einsum('hdk,hkj->hdj', xh, a).reshape(C, N) + f64(bo)
    out = f64(base).copy()
    out[:, idx] = f64(x) + y
    return out

@@ -1,0 +1,126 @@
+import math
+
+import concourse.mybir as mybir
+from concourse.masks import make_identity
+
+F32 = mybir.dt.float32
+BF16 = mybir.dt.bfloat16
+U16 = mybir.dt.uint16
+ADD = mybir.AluOpType.add
+MULT = mybir.AluOpType.mult
+EXP = mybir.ActivationFunctionType.Exp
+IDENTITY = mybir.ActivationFunctionType.Identity
+ALONG_ROW = mybir.AxisListType.X
+
+P = 128
+HEADS = 2
+NODES = 256
+SLOTS = 512
+BLOCKS = NODES // P
+SCALE = 1.0 / math.sqrt(P)
+NO_EDGE = -32768.0
+
+FLOPS = 4 * HEADS * P * NODES * NODES
+
+
+def block(i):
+    return slice(i * P, (i + 1) * P)
+
+
+def tile_gat_kernel(tc, base, x, adj_t, bo, offs, out):
+    nc = tc.nc
+    with (
+        tc.tile_pool(name="held", bufs=1) as held,
+        tc.tile_pool(name="rows", bufs=HEADS * BLOCKS) as rows,
+        tc.psum_pool(name="score_banks", bufs=HEADS * BLOCKS) as score_banks,
+        tc.psum_pool(name="flipped_banks", bufs=2) as flipped_banks,
+        tc.psum_pool(name="sum_banks", bufs=HEADS) as sum_banks,
+    ):
+        queues = (nc.sync, nc.scalar)
+        x_f32 = [held.tile([P, NODES], F32, name=f"x_f32_{h}") for h in range(HEADS)]
+        adj = [held.tile([P, NODES], F32, name=f"adj_{kb}") for kb in range(BLOCKS)]
+        window = [held.tile([P, SLOTS], F32, name=f"window_{h}") for h in range(HEADS)]
+        bias = [held.tile([P, 1], F32, name=f"bias_{h}") for h in range(HEADS)]
+        offsets = held.tile([P, NODES // 16], U16, name="offsets")
+        for h in range(HEADS):
+            queues[h].dma_start(x_f32[h][:], x[block(h), :])
+        for kb in range(BLOCKS):
+            queues[kb].dma_start(adj[kb][:], adj_t[block(kb), :])
+        nc.sync.dma_start(offsets[:], offs)
+        for h in range(HEADS):
+            queues[h].dma_start(window[h][:], base[block(h), :])
+            nc.gpsimd.dma_start(bias[h][:], bo[block(h), :])
+
+        warm = held.tile([P, 1], F32, name="warm")
+        nc.vector.memset(warm[:], 0.0)
+        nc.scalar.activation(warm[:], warm[:], EXP)
+
+        identity = held.tile([P, P], BF16, name="identity")
+        make_identity(nc, identity[:])
+
+        x_bf16 = [held.tile([P, NODES], BF16, name=f"x_bf16_{h}") for h in range(HEADS)]
+        no_edge = [held.tile([P, NODES], BF16, name=f"no_edge_{kb}") for kb in range(BLOCKS)]
+        for h in range(HEADS):
+            nc.vector.tensor_copy(x_bf16[h][:], x_f32[h][:])
+        for kb in range(BLOCKS):
+            nc.gpsimd.tensor_scalar(no_edge[kb][:], adj[kb][:], -NO_EDGE, NO_EDGE, MULT, ADD)
+
+        scores = {}
+        for h in range(HEADS):
+            for jb in range(BLOCKS):
+                scores[h, jb] = score_banks.tile([P, NODES], F32, name="scores")
+                nc.tensor.matmul(scores[h, jb][:], x_bf16[h][:, block(jb)], x_bf16[h][:], start=True, stop=False)
+                for kb in range(BLOCKS):
+                    nc.tensor.matmul(
+                        scores[h, jb][:, block(kb)],
+                        no_edge[kb][:, block(jb)],
+                        identity[:],
+                        start=False,
+                        stop=(kb == BLOCKS - 1),
+                    )
+
+        x_t_bank = flipped_banks.tile([P, BLOCKS * HEADS * P], BF16, name="flipped")
+        for kb in range(BLOCKS):
+            for h in range(HEADS):
+                nc.tensor.transpose(x_t_bank[:, block(kb * HEADS + h)], x_bf16[h][:, block(kb)], identity[:])
+        x_t = held.tile([P, BLOCKS * HEADS * P], BF16, name="x_t")
+        nc.scalar.copy(x_t[:], x_t_bank[:])
+
+        weights_t_bank = {}
+        for h in range(HEADS):
+            weights_t_bank[h] = flipped_banks.tile([P, BLOCKS * NODES], BF16, name="flipped")
+            for jb in range(BLOCKS):
+                neg_max = rows.tile([P, 1], F32, name="neg_max")
+                nc.vector.reduce_max(neg_max[:], scores[h, jb][:], axis=ALONG_ROW, negate=True)
+                shift = rows.tile([P, 1], F32, name="shift")
+                nc.vector.tensor_scalar_mul(shift[:], neg_max[:], SCALE)
+                e = rows.tile([P, NODES], F32, name="e")
+                total = rows.tile([P, 1], F32, name="total")
+                nc.scalar.activation(e[:], scores[h, jb][:], EXP, bias=shift[:], scale=SCALE, accum_out=total[:])
+                inverse = rows.tile([P, 1], F32, name="inverse")
+                nc.vector.reciprocal(inverse[:], total[:])
+                weights = rows.tile([P, NODES], BF16, name="weights")
+                nc.vector.tensor_scalar_mul(weights[:], e[:], inverse[:])
+                for kb in range(BLOCKS):
+                    nc.tensor.transpose(
+                        weights_t_bank[h][:, block(kb * BLOCKS + jb)], weights[:, block(kb)], identity[:]
+                    )
+
+        y = {}
+        for h in range(HEADS):
+            weights_t = rows.tile([P, BLOCKS * NODES], BF16, name="weights_t")
+            nc.scalar.copy(weights_t[:], weights_t_bank[h][:])
+            weighted = sum_banks.tile([P, NODES], F32, name="weighted")
+            for kb in range(BLOCKS):
+                nc.tensor.matmul(
+                    weighted[:],
+                    x_t[:, block(kb * HEADS + h)],
+                    weights_t[:, kb * NODES : (kb + 1) * NODES],
+                    start=(kb == 0),
+                    stop=(kb == BLOCKS - 1),
+                )
+            y[h] = rows.tile([P, NODES], F32, name="y")
+            nc.scalar.activation(y[h][:], weighted[:], IDENTITY, bias=bias[h][:])
+        for h in range(HEADS):
+            nc.vector.tensor_tensor(window[h][:].indirect(offsets[:]), x_f32[h][:], y[h][:], ADD)
+            queues[h].dma_start(out[block(h), :], window[h][:])

@@ -49,7 +49,8 @@ def tile_gat_kernel(tc, base, x, adj_t, bo, offs, out):
         nc.sync.dma_start(offsets[:], offs)
         for h in range(HEADS):
             queues[h].dma_start(window[h][:], base[block(h), :])
-            nc.gpsimd.dma_start(bias[h][:], bo[block(h), :])
+        for h in range(HEADS):
+            queues[h].dma_start(bias[h][:], bo[block(h), :])
 
         warm = held.tile([P, 1], F32, name="warm")
         nc.vector.memset(warm[:], 0.0)
@@ -63,7 +64,7 @@ def tile_gat_kernel(tc, base, x, adj_t, bo, offs, out):
         for h in range(HEADS):
             nc.vector.tensor_copy(x_bf16[h][:], x_f32[h][:])
         for kb in range(BLOCKS):
-            nc.gpsimd.tensor_scalar(no_edge[kb][:], adj[kb][:], -NO_EDGE, NO_EDGE, MULT, ADD)
+            nc.vector.tensor_scalar(no_edge[kb][:], adj[kb][:], -NO_EDGE, NO_EDGE, MULT, ADD)
 
         scores = {}
         for h in range(HEADS):

@@ -8,9 +8,9 @@ BF16 = mybir.dt.bfloat16
 U16 = mybir.dt.uint16
 ADD = mybir.AluOpType.add
 MULT = mybir.AluOpType.mult
+MIN = mybir.AluOpType.min
 EXP = mybir.ActivationFunctionType.Exp
 IDENTITY = mybir.ActivationFunctionType.Identity
-ALONG_ROW = mybir.AxisListType.X
 
 P = 128
 HEADS = 2
@@ -38,14 +38,14 @@ def tile_gat_kernel(tc, base, x, adj_t, bo, offs, out):
     ):
         queues = (nc.sync, nc.scalar)
         x_f32 = [held.tile([P, NODES], F32, name=f"x_f32_{h}") for h in range(HEADS)]
-        adj = [held.tile([P, NODES], F32, name=f"adj_{kb}") for kb in range(BLOCKS)]
+        adj = [held.tile([P, BLOCKS, P], F32, name=f"adj_{jb}") for jb in range(BLOCKS)]
         window = [held.tile([P, SLOTS], F32, name=f"window_{h}") for h in range(HEADS)]
         bias = [held.tile([P, 1], F32, name=f"bias_{h}") for h in range(HEADS)]
         offsets = held.tile([P, NODES // 16], U16, name="offsets")
-        for h in range(HEADS):
-            queues[h].dma_start(x_f32[h][:], x[block(h), :])
-        for kb in range(BLOCKS):
-            queues[kb].dma_start(adj[kb][:], adj_t[block(kb), :])
+        nc.sync.dma_start(x_f32[0][:], x[block(0), :])
+        nc.scalar.dma_start(adj[0][:], adj_t[:, block(0)].rearrange("(kb p) j -> p kb j", p=P))
+        nc.sync.dma_start(adj[1][:], adj_t[:, block(1)].rearrange("(kb p) j -> p kb j", p=P))
+        nc.scalar.dma_start(x_f32[1][:], x[block(1), :])
         nc.sync.dma_start(offsets[:], offs)
         for h in range(HEADS):
             queues[h].dma_start(window[h][:], base[block(h), :])
@@ -60,25 +60,11 @@ def tile_gat_kernel(tc, base, x, adj_t, bo, offs, out):
         make_identity(nc, identity[:])
 
         x_bf16 = [held.tile([P, NODES], BF16, name=f"x_bf16_{h}") for h in range(HEADS)]
-        no_edge = [held.tile([P, NODES], BF16, name=f"no_edge_{kb}") for kb in range(BLOCKS)]
-        for h in range(HEADS):
-            nc.vector.tensor_copy(x_bf16[h][:], x_f32[h][:])
-        for kb in range(BLOCKS):
-            nc.vector.tensor_scalar(no_edge[kb][:], adj[kb][:], -NO_EDGE, NO_EDGE, MULT, ADD)
-
-        scores = {}
-        for h in range(HEADS):
-            for jb in range(BLOCKS):
-                scores[h, jb] = score_banks.tile([P, NODES], F32, name="scores")
-                nc.tensor.matmul(scores[h, jb][:], x_bf16[h][:, block(jb)], x_bf16[h][:], start=True, stop=False)
-                for kb in range(BLOCKS):
-                    nc.tensor.matmul(
-                        scores[h, jb][:, block(kb)],
-                        no_edge[kb][:, block(jb)],
-                        identity[:],
-                        start=False,
-                        stop=(kb == BLOCKS - 1),
-                    )
+        no_edge = [held.tile([P, BLOCKS, P], BF16, name=f"no_edge_{jb}") for jb in range(BLOCKS)]
+        nc.vector.tensor_copy(x_bf16[0][:], x_f32[0][:])
+        for jb in range(BLOCKS):
+            nc.vector.tensor_scalar(no_edge[jb][:], adj[jb][:], -NO_EDGE, NO_EDGE, MULT, ADD)
+        nc.vector.tensor_copy(x_bf16[1][:], x_f32[1][:])
 
         x_t_bank = flipped_banks.tile([P, BLOCKS * HEADS * P], BF16, name="flipped")
         for kb in range(BLOCKS):
@@ -87,41 +73,46 @@ def tile_gat_kernel(tc, base, x, adj_t, bo, offs, out):
         x_t = held.tile([P, BLOCKS * HEADS * P], BF16, name="x_t")
         nc.scalar.copy(x_t[:], x_t_bank[:])
 
-        weights_t_bank = {}
+        y = {}
         for h in range(HEADS):
-            weights_t_bank[h] = flipped_banks.tile([P, BLOCKS * NODES], BF16, name="flipped")
+            weighted = sum_banks.tile([P, NODES], F32, name="weighted")
             for jb in range(BLOCKS):
-                neg_max = rows.tile([P, 1], F32, name="neg_max")
-                nc.vector.reduce_max(neg_max[:], scores[h, jb][:], axis=ALONG_ROW, negate=True)
+                scores = score_banks.tile([P, NODES], F32, name="scores")
+                nc.tensor.matmul(scores[:], x_bf16[h][:, block(jb)], x_bf16[h][:], start=True, stop=False)
+                for kb in range(BLOCKS):
+                    nc.tensor.matmul(
+                        scores[:, block(kb)],
+                        no_edge[jb][:, kb, :],
+                        identity[:],
+                        start=False,
+                        stop=(kb == BLOCKS - 1),
+                    )
+                negated = rows.tile([P, NODES], F32, name="negated")
                 shift = rows.tile([P, 1], F32, name="shift")
-                nc.vector.tensor_scalar_mul(shift[:], neg_max[:], SCALE)
+                nc.vector.tensor_scalar(negated[:], scores[:], -SCALE, None, MULT, MIN, accum_out=shift[:])
                 e = rows.tile([P, NODES], F32, name="e")
                 total = rows.tile([P, 1], F32, name="total")
-                nc.scalar.activation(e[:], scores[h, jb][:], EXP, bias=shift[:], scale=SCALE, accum_out=total[:])
+                nc.scalar.activation(e[:], negated[:], EXP, bias=shift[:], scale=-1.0, accum_out=total[:])
                 inverse = rows.tile([P, 1], F32, name="inverse")
                 nc.vector.reciprocal(inverse[:], total[:])
                 weights = rows.tile([P, NODES], BF16, name="weights")
                 nc.vector.tensor_scalar_mul(weights[:], e[:], inverse[:])
+                weights_t_bank = flipped_banks.tile([P, NODES], BF16, name="flipped")
                 for kb in range(BLOCKS):
-                    nc.tensor.transpose(
-                        weights_t_bank[h][:, block(kb * BLOCKS + jb)], weights[:, block(kb)], identity[:]
+                    nc.tensor.transpose(weights_t_bank[:, block(kb)], weights[:, block(kb)], identity[:])
+                weights_t = rows.tile([P, NODES], BF16, name="weights_t")
+                nc.scalar.copy(weights_t[:], weights_t_bank[:])
+                for kb in range(BLOCKS):
+                    nc.tensor.matmul(
+                        weighted[:, block(jb)],
+                        x_t[:, block(kb * HEADS + h)],
+                        weights_t[:, block(kb)],
+                        start=(kb == 0),
+                        stop=(kb == BLOCKS - 1),
                     )
-
-        y = {}
-        for h in range(HEADS):
-            weights_t = rows.tile([P, BLOCKS * NODES], BF16, name="weights_t")
-            nc.scalar.copy(weights_t[:], weights_t_bank[h][:])
-            weighted = sum_banks.tile([P, NODES], F32, name="weighted")
-            for kb in range(BLOCKS):
-                nc.tensor.matmul(
-                    weighted[:],
-                    x_t[:, block(kb * HEADS + h)],
-                    weights_t[:, kb * NODES : (kb + 1) * NODES],
-                    start=(kb == 0),
-                    stop=(kb == BLOCKS - 1),
-                )
             y[h] = rows.tile([P, NODES], F32, name="y")
             nc.scalar.activation(y[h][:], weighted[:], IDENTITY, bias=bias[h][:])
+
         for h in range(HEADS):
             nc.vector.tensor_tensor(window[h][:].indirect(offsets[:]), x_f32[h][:], y[h][:], ADD)
             queues[h].dma_start(out[block(h), :], window[h][:])

@@ -66,30 +66,32 @@ def tile_gat_kernel(tc, base, x, adj_t, bo, offs, out):
             nc.vector.tensor_scalar(no_edge[jb][:], adj[jb][:], -NO_EDGE, NO_EDGE, MULT, ADD)
         nc.vector.tensor_copy(x_bf16[1][:], x_f32[1][:])
 
-        x_t_bank = flipped_banks.tile([P, BLOCKS * HEADS * P], BF16, name="flipped")
-        for kb in range(BLOCKS):
-            for h in range(HEADS):
-                nc.tensor.transpose(x_t_bank[:, block(kb * HEADS + h)], x_bf16[h][:, block(kb)], identity[:])
-        x_t = held.tile([P, BLOCKS * HEADS * P], BF16, name="x_t")
-        nc.scalar.copy(x_t[:], x_t_bank[:])
-
-        y = {}
+        scores = {}
         for h in range(HEADS):
-            weighted = sum_banks.tile([P, NODES], F32, name="weighted")
             for jb in range(BLOCKS):
-                scores = score_banks.tile([P, NODES], F32, name="scores")
-                nc.tensor.matmul(scores[:], x_bf16[h][:, block(jb)], x_bf16[h][:], start=True, stop=False)
+                scores[h, jb] = score_banks.tile([P, NODES], F32, name="scores")
+                nc.tensor.matmul(scores[h, jb][:], x_bf16[h][:, block(jb)], x_bf16[h][:], start=True, stop=False)
                 for kb in range(BLOCKS):
                     nc.tensor.matmul(
-                        scores[:, block(kb)],
+                        scores[h, jb][:, block(kb)],
                         no_edge[jb][:, kb, :],
                         identity[:],
                         start=False,
                         stop=(kb == BLOCKS - 1),
                     )
+
+        y = {}
+        for h in range(HEADS):
+            x_t_bank = flipped_banks.tile([P, NODES], BF16, name="flipped")
+            for kb in range(BLOCKS):
+                nc.tensor.transpose(x_t_bank[:, block(kb)], x_bf16[h][:, block(kb)], identity[:])
+            x_t = rows.tile([P, NODES], BF16, name="x_t")
+            nc.scalar.copy(x_t[:], x_t_bank[:])
+            weighted = sum_banks.tile([P, NODES], F32, name="weighted")
+            for jb in range(BLOCKS):
                 negated = rows.tile([P, NODES], F32, name="negated")
                 shift = rows.tile([P, 1], F32, name="shift")
-                nc.vector.tensor_scalar(negated[:], scores[:], -SCALE, None, MULT, MIN, accum_out=shift[:])
+                nc.vector.tensor_scalar(negated[:], scores[h, jb][:], -SCALE, None, MULT, MIN, accum_out=shift[:])
                 e = rows.tile([P, NODES], F32, name="e")
                 total = rows.tile([P, 1], F32, name="total")
                 nc.scalar.activation(e[:], negated[:], EXP, bias=shift[:], scale=-1.0, accum_out=total[:])
@@ -105,7 +107,7 @@ def tile_gat_kernel(tc, base, x, adj_t, bo, offs, out):
                 for kb in range(BLOCKS):
                     nc.tensor.matmul(
                         weighted[:, block(jb)],
-                        x_t[:, block(kb * HEADS + h)],
+                        x_t[:, block(kb)],
                         weights_t[:, block(kb)],
                         start=(kb == 0),
                         stop=(kb == BLOCKS - 1),

@@ -46,11 +46,11 @@ def tile_gat_kernel(tc, base, x, adj_t, bo, offs, out):
         nc.scalar.dma_start(adj[0][:], adj_t[:, block(0)].rearrange("(kb p) j -> p kb j", p=P))
         nc.sync.dma_start(adj[1][:], adj_t[:, block(1)].rearrange("(kb p) j -> p kb j", p=P))
         nc.scalar.dma_start(x_f32[1][:], x[block(1), :])
+        for h in range(HEADS):
+            queues[h].dma_start(bias[h][:], bo[block(h), :])
         nc.sync.dma_start(offsets[:], offs)
         for h in range(HEADS):
             queues[h].dma_start(window[h][:], base[block(h), :])
-        for h in range(HEADS):
-            queues[h].dma_start(bias[h][:], bo[block(h), :])
 
         warm = held.tile([P, 1], F32, name="warm")
         nc.vector.memset(warm[:], 0.0)

@@ -45,12 +45,12 @@ def tile_gat_kernel(tc, base, x, adj_t, bo, offs, out):
         nc.sync.dma_start(x_f32[0][:], x[block(0), :])
         nc.scalar.dma_start(adj[0][:], adj_t[:, block(0)].rearrange("(kb p) j -> p kb j", p=P))
         nc.sync.dma_start(adj[1][:], adj_t[:, block(1)].rearrange("(kb p) j -> p kb j", p=P))
-        nc.scalar.dma_start(x_f32[1][:], x[block(1), :])
+        nc.sync.dma_start(x_f32[1][:], x[block(1), :])
         for h in range(HEADS):
-            queues[h].dma_start(bias[h][:], bo[block(h), :])
+            nc.sync.dma_start(bias[h][:], bo[block(h), :])
         nc.sync.dma_start(offsets[:], offs)
         for h in range(HEADS):
-            queues[h].dma_start(window[h][:], base[block(h), :])
+            nc.sync.dma_start(window[h][:], base[block(h), :])
 
         warm = held.tile([P, 1], F32, name="warm")
         nc.vector.memset(warm[:], 0.0)

@@ -20,6 +20,8 @@ BLOCKS = NODES // P
 SCALE = 1.0 / math.sqrt(P)
 NO_EDGE = -32768.0
 
+WARMING_MATMULS = 12
+
 FLOPS = 4 * HEADS * P * NODES * NODES
 
 
@@ -45,12 +47,12 @@ def tile_gat_kernel(tc, base, x, adj_t, bo, offs, out):
         nc.sync.dma_start(x_f32[0][:], x[block(0), :])
         nc.scalar.dma_start(adj[0][:], adj_t[:, block(0)].rearrange("(kb p) j -> p kb j", p=P))
         nc.sync.dma_start(adj[1][:], adj_t[:, block(1)].rearrange("(kb p) j -> p kb j", p=P))
-        nc.sync.dma_start(x_f32[1][:], x[block(1), :])
+        nc.scalar.dma_start(x_f32[1][:], x[block(1), :])
         for h in range(HEADS):
-            nc.sync.dma_start(bias[h][:], bo[block(h), :])
+            queues[h].dma_start(bias[h][:], bo[block(h), :])
         nc.sync.dma_start(offsets[:], offs)
         for h in range(HEADS):
-            nc.sync.dma_start(window[h][:], base[block(h), :])
+            queues[h].dma_start(window[h][:], base[block(h), :])
 
         warm = held.tile([P, 1], F32, name="warm")
         nc.vector.memset(warm[:], 0.0)
@@ -58,6 +60,10 @@ def tile_gat_kernel(tc, base, x, adj_t, bo, offs, out):
 
         identity = held.tile([P, P], BF16, name="identity")
         make_identity(nc, identity[:])
+
+        idle_bank = score_banks.tile([P, P], F32, name="scores")
+        for i in range(WARMING_MATMULS):
+            nc.tensor.matmul(idle_bank[:], identity[:], identity[:], start=True, stop=True)
 
         x_bf16 = [held.tile([P, NODES], BF16, name=f"x_bf16_{h}") for h in range(HEADS)]
         no_edge = [held.tile([P, BLOCKS, P], BF16, name=f"no_edge_{jb}") for jb in range(BLOCKS)]

@@ -21,6 +21,7 @@ SCALE = 1.0 / math.sqrt(P)
 NO_EDGE = -32768.0
 
 WARMING_MATMULS = 12
+WAITING_MATMULS = 12
 
 FLOPS = 4 * HEADS * P * NODES * NODES
 
@@ -86,13 +87,19 @@ def tile_gat_kernel(tc, base, x, adj_t, bo, offs, out):
                         stop=(kb == BLOCKS - 1),
                     )
 
-        y = {}
+        x_t = [held.tile([P, NODES], BF16, name=f"x_t_{h}") for h in range(HEADS)]
         for h in range(HEADS):
             x_t_bank = flipped_banks.tile([P, NODES], BF16, name="flipped")
             for kb in range(BLOCKS):
                 nc.tensor.transpose(x_t_bank[:, block(kb)], x_bf16[h][:, block(kb)], identity[:])
-            x_t = rows.tile([P, NODES], BF16, name="x_t")
-            nc.scalar.copy(x_t[:], x_t_bank[:])
+            nc.scalar.copy(x_t[h][:], x_t_bank[:])
+
+        waiting_bank = sum_banks.tile([P, P], F32, name="waiting_bank", tag="weighted")
+        for i in range(WAITING_MATMULS):
+            nc.tensor.matmul(waiting_bank[:], identity[:], identity[:], start=True, stop=True)
+
+        y = {}
+        for h in range(HEADS):
             weighted = sum_banks.tile([P, NODES], F32, name="weighted")
             for jb in range(BLOCKS):
                 negated = rows.tile([P, NODES], F32, name="negated")
@@ -113,7 +120,7 @@ def tile_gat_kernel(tc, base, x, adj_t, bo, offs, out):
                 for kb in range(BLOCKS):
                     nc.tensor.matmul(
                         weighted[:, block(jb)],
-                        x_t[:, block(kb)],
+                        x_t[h][:, block(kb)],
                         weights_t[:, block(kb)],
                         start=(kb == 0),
                         stop=(kb == BLOCKS - 1),

@@ -91,7 +91,7 @@ def tile_gat_kernel(tc, base, x, adj_t, bo, offs, out):
         for h in range(HEADS):
             x_t_bank = flipped_banks.tile([P, NODES], BF16, name="flipped")
             for kb in range(BLOCKS):
-                nc.tensor.transpose(x_t_bank[:, block(kb)], x_bf16[h][:, block(kb)], identity[:])
+                nc.tensor.matmul(x_t_bank[:, block(kb)], x_bf16[h][:, block(kb)], identity[:], start=True, stop=True)
             nc.scalar.copy(x_t[h][:], x_t_bank[:])
 
         waiting_bank = sum_banks.tile([P, P], F32, name="waiting_bank", tag="weighted")
@@ -114,7 +114,9 @@ def tile_gat_kernel(tc, base, x, adj_t, bo, offs, out):
                 nc.vector.tensor_scalar_mul(weights[:], e[:], inverse[:])
                 weights_t_bank = flipped_banks.tile([P, NODES], BF16, name="flipped")
                 for kb in range(BLOCKS):
-                    nc.tensor.transpose(weights_t_bank[:, block(kb)], weights[:, block(kb)], identity[:])
+                    nc.tensor.matmul(
+                        weights_t_bank[:, block(kb)], weights[:, block(kb)], identity[:], start=True, stop=True
+                    )
                 weights_t = rows.tile([P, NODES], BF16, name="weights_t")
                 nc.scalar.copy(weights_t[:], weights_t_bank[:])
                 for kb in range(BLOCKS):

@@ -100,7 +100,7 @@ def tile_gat_kernel(tc, base, x, adj_t, bo, offs, out):
 
         y = {}
         for h in range(HEADS):
-            weighted = sum_banks.tile([P, NODES], F32, name="weighted")
+            y[h] = rows.tile([P, NODES], F32, name="y")
             for jb in range(BLOCKS):
                 negated = rows.tile([P, NODES], F32, name="negated")
                 shift = rows.tile([P, 1], F32, name="shift")
@@ -119,16 +119,16 @@ def tile_gat_kernel(tc, base, x, adj_t, bo, offs, out):
                     )
                 weights_t = rows.tile([P, NODES], BF16, name="weights_t")
                 nc.scalar.copy(weights_t[:], weights_t_bank[:])
+                weighted = sum_banks.tile([P, P], F32, name="weighted")
                 for kb in range(BLOCKS):
                     nc.tensor.matmul(
-                        weighted[:, block(jb)],
+                        weighted[:],
                         x_t[h][:, block(kb)],
                         weights_t[:, block(kb)],
                         start=(kb == 0),
                         stop=(kb == BLOCKS - 1),
                     )
-            y[h] = rows.tile([P, NODES], F32, name="y")
-            nc.scalar.activation(y[h][:], weighted[:], IDENTITY, bias=bias[h][:])
+                nc.scalar.activation(y[h][:, block(jb)], weighted[:], IDENTITY, bias=bias[h][:])
 
         for h in range(HEADS):
             nc.vector.tensor_tensor(window[h][:].indirect(offsets[:]), x_f32[h][:], y[h][:], ADD)

@@ -118,7 +118,10 @@ def tile_gat_kernel(tc, base, x, adj_t, bo, offs, out):
                         weights_t_bank[:, block(kb)], weights[:, block(kb)], identity[:], start=True, stop=True
                     )
                 weights_t = rows.tile([P, NODES], BF16, name="weights_t")
-                nc.scalar.copy(weights_t[:], weights_t_bank[:])
+                if h == 0:
+                    nc.vector.tensor_copy(weights_t[:], weights_t_bank[:])
+                else:
+                    nc.scalar.copy(weights_t[:], weights_t_bank[:])
                 weighted = sum_banks.tile([P, P], F32, name="weighted")
                 for kb in range(BLOCKS):
                     nc.tensor.matmul(

@@ -20,7 +20,8 @@ BLOCKS = NODES // P
 SCALE = 1.0 / math.sqrt(P)
 NO_EDGE = -32768.0
 
-WARMING_MATMULS = 12
+WARMING_ROWS = 32
+WARMING_MATMULS = 14
 WAITING_MATMULS = 12
 
 FLOPS = 4 * HEADS * P * NODES * NODES
@@ -35,18 +36,22 @@ def tile_gat_kernel(tc, base, x, adj_t, bo, offs, out):
     with (
         tc.tile_pool(name="held", bufs=1) as held,
         tc.tile_pool(name="rows", bufs=HEADS * BLOCKS) as rows,
+        tc.tile_pool(name="negated_ring", bufs=BLOCKS) as negated_ring,
         tc.psum_pool(name="score_banks", bufs=HEADS * BLOCKS) as score_banks,
         tc.psum_pool(name="flipped_banks", bufs=2) as flipped_banks,
         tc.psum_pool(name="sum_banks", bufs=HEADS) as sum_banks,
     ):
+        zeros = held.tile([P, WARMING_ROWS], BF16, name="zeros")
+        nc.vector.memset(zeros[:], 0.0)
+
         queues = (nc.sync, nc.scalar)
         x_f32 = [held.tile([P, NODES], F32, name=f"x_f32_{h}") for h in range(HEADS)]
         adj = [held.tile([P, BLOCKS, P], F32, name=f"adj_{jb}") for jb in range(BLOCKS)]
         window = [held.tile([P, SLOTS], F32, name=f"window_{h}") for h in range(HEADS)]
         bias = [held.tile([P, 1], F32, name=f"bias_{h}") for h in range(HEADS)]
         offsets = held.tile([P, NODES // 16], U16, name="offsets")
-        nc.sync.dma_start(x_f32[0][:], x[block(0), :])
-        nc.scalar.dma_start(adj[0][:], adj_t[:, block(0)].rearrange("(kb p) j -> p kb j", p=P))
+        nc.sync.dma_start(adj[0][:], adj_t[:, block(0)].rearrange("(kb p) j -> p kb j", p=P))
+        nc.scalar.dma_start(x_f32[0][:], x[block(0), :])
         nc.sync.dma_start(adj[1][:], adj_t[:, block(1)].rearrange("(kb p) j -> p kb j", p=P))
         nc.scalar.dma_start(x_f32[1][:], x[block(1), :])
         for h in range(HEADS):
@@ -56,36 +61,32 @@ def tile_gat_kernel(tc, base, x, adj_t, bo, offs, out):
             queues[h].dma_start(window[h][:], base[block(h), :])
 
         warm = held.tile([P, 1], F32, name="warm")
-        nc.vector.memset(warm[:], 0.0)
-        nc.scalar.activation(warm[:], warm[:], EXP)
+        nc.scalar.activation(warm[:], zeros[:, 0:1], EXP)
 
         identity = held.tile([P, P], BF16, name="identity")
         make_identity(nc, identity[:])
 
         idle_bank = score_banks.tile([P, P], F32, name="scores")
         for i in range(WARMING_MATMULS):
-            nc.tensor.matmul(idle_bank[:], identity[:], identity[:], start=True, stop=True)
+            nc.tensor.matmul(
+                idle_bank[:WARMING_ROWS, :], zeros[:], zeros[:, 0:1].to_broadcast([P, P]), start=True, stop=True
+            )
 
         x_bf16 = [held.tile([P, NODES], BF16, name=f"x_bf16_{h}") for h in range(HEADS)]
         no_edge = [held.tile([P, BLOCKS, P], BF16, name=f"no_edge_{jb}") for jb in range(BLOCKS)]
-        nc.vector.tensor_copy(x_bf16[0][:], x_f32[0][:])
-        for jb in range(BLOCKS):
-            nc.vector.tensor_scalar(no_edge[jb][:], adj[jb][:], -NO_EDGE, NO_EDGE, MULT, ADD)
-        nc.vector.tensor_copy(x_bf16[1][:], x_f32[1][:])
+        for i in range(HEADS):
+            nc.vector.tensor_scalar(no_edge[i][:], adj[i][:], -NO_EDGE, NO_EDGE, MULT, ADD)
+            nc.vector.tensor_copy(x_bf16[i][:], x_f32[i][:])
 
         scores = {}
         for h in range(HEADS):
             for jb in range(BLOCKS):
                 scores[h, jb] = score_banks.tile([P, NODES], F32, name="scores")
-                nc.tensor.matmul(scores[h, jb][:], x_bf16[h][:, block(jb)], x_bf16[h][:], start=True, stop=False)
                 for kb in range(BLOCKS):
                     nc.tensor.matmul(
-                        scores[h, jb][:, block(kb)],
-                        no_edge[jb][:, kb, :],
-                        identity[:],
-                        start=False,
-                        stop=(kb == BLOCKS - 1),
+                        scores[h, jb][:, block(kb)], no_edge[jb][:, kb, :], identity[:], start=(kb == 0), stop=False
                     )
+                nc.tensor.matmul(scores[h, jb][:], x_bf16[h][:, block(jb)], x_bf16[h][:], start=False, stop=True)
 
         x_t = [held.tile([P, NODES], BF16, name=f"x_t_{h}") for h in range(HEADS)]
         for h in range(HEADS):
@@ -102,7 +103,7 @@ def tile_gat_kernel(tc, base, x, adj_t, bo, offs, out):
         for h in range(HEADS):
             y[h] = rows.tile([P, NODES], F32, name="y")
             for jb in range(BLOCKS):
-                negated = rows.tile([P, NODES], F32, name="negated")
+                negated = negated_ring.tile([P, NODES], F32, name="negated")
                 shift = rows.tile([P, 1], F32, name="shift")
                 nc.vector.tensor_scalar(negated[:], scores[h, jb][:], -SCALE, None, MULT, MIN, accum_out=shift[:])
                 e = rows.tile([P, NODES], F32, name="e")

@@ -9,6 +9,7 @@ U16 = mybir.dt.uint16
 ADD = mybir.AluOpType.add
 MULT = mybir.AluOpType.mult
 MIN = mybir.AluOpType.min
+SUBTRACT = mybir.AluOpType.subtract
 EXP = mybir.ActivationFunctionType.Exp
 IDENTITY = mybir.ActivationFunctionType.Identity
 
@@ -22,7 +23,6 @@ NO_EDGE = -32768.0
 
 WARMING_ROWS = 32
 WARMING_MATMULS = 14
-WAITING_MATMULS = 12
 
 FLOPS = 4 * HEADS * P * NODES * NODES
 
@@ -36,7 +36,6 @@ def tile_gat_kernel(tc, base, x, adj_t, bo, offs, out):
     with (
         tc.tile_pool(name="held", bufs=1) as held,
         tc.tile_pool(name="rows", bufs=HEADS * BLOCKS) as rows,
-        tc.tile_pool(name="negated_ring", bufs=BLOCKS) as negated_ring,
         tc.psum_pool(name="score_banks", bufs=HEADS * BLOCKS) as score_banks,
         tc.psum_pool(name="flipped_banks", bufs=2) as flipped_banks,
         tc.psum_pool(name="sum_banks", bufs=HEADS) as sum_banks,
@@ -88,52 +87,95 @@ def tile_gat_kernel(tc, base, x, adj_t, bo, offs, out):
                     )
                 nc.tensor.matmul(scores[h, jb][:], x_bf16[h][:, block(jb)], x_bf16[h][:], start=False, stop=True)
 
-        x_t = [held.tile([P, NODES], BF16, name=f"x_t_{h}") for h in range(HEADS)]
+        x_bias = held.tile([P, NODES], F32, name="x_bias")
+        nc.scalar.activation(x_bias[:], x_f32[0][:], IDENTITY, bias=bias[0][:])
+        e, total = {}, {}
         for h in range(HEADS):
-            x_t_bank = flipped_banks.tile([P, NODES], BF16, name="flipped")
-            for kb in range(BLOCKS):
-                nc.tensor.matmul(x_t_bank[:, block(kb)], x_bf16[h][:, block(kb)], identity[:], start=True, stop=True)
-            nc.scalar.copy(x_t[h][:], x_t_bank[:])
-
-        waiting_bank = sum_banks.tile([P, P], F32, name="waiting_bank", tag="weighted")
-        for i in range(WAITING_MATMULS):
-            nc.tensor.matmul(waiting_bank[:], identity[:], identity[:], start=True, stop=True)
-
-        y = {}
-        for h in range(HEADS):
-            y[h] = rows.tile([P, NODES], F32, name="y")
+            total[h] = held.tile([P, BLOCKS], F32, name=f"total_{h}")
             for jb in range(BLOCKS):
-                negated = negated_ring.tile([P, NODES], F32, name="negated")
+                negated = rows.tile([P, NODES], F32, name="negated")
                 shift = rows.tile([P, 1], F32, name="shift")
                 nc.vector.tensor_scalar(negated[:], scores[h, jb][:], -SCALE, None, MULT, MIN, accum_out=shift[:])
-                e = rows.tile([P, NODES], F32, name="e")
-                total = rows.tile([P, 1], F32, name="total")
-                nc.scalar.activation(e[:], negated[:], EXP, bias=shift[:], scale=-1.0, accum_out=total[:])
-                inverse = rows.tile([P, 1], F32, name="inverse")
-                nc.vector.reciprocal(inverse[:], total[:])
-                weights = rows.tile([P, NODES], BF16, name="weights")
-                nc.vector.tensor_scalar_mul(weights[:], e[:], inverse[:])
-                weights_t_bank = flipped_banks.tile([P, NODES], BF16, name="flipped")
-                for kb in range(BLOCKS):
-                    nc.tensor.matmul(
-                        weights_t_bank[:, block(kb)], weights[:, block(kb)], identity[:], start=True, stop=True
-                    )
-                weights_t = rows.tile([P, NODES], BF16, name="weights_t")
-                if h == 0:
-                    nc.vector.tensor_copy(weights_t[:], weights_t_bank[:])
-                else:
-                    nc.scalar.copy(weights_t[:], weights_t_bank[:])
-                weighted = sum_banks.tile([P, P], F32, name="weighted")
-                for kb in range(BLOCKS):
-                    nc.tensor.matmul(
-                        weighted[:],
-                        x_t[h][:, block(kb)],
-                        weights_t[:, block(kb)],
-                        start=(kb == 0),
-                        stop=(kb == BLOCKS - 1),
-                    )
-                nc.scalar.activation(y[h][:, block(jb)], weighted[:], IDENTITY, bias=bias[h][:])
+                e[h, jb] = rows.tile([P, NODES], BF16 if h == 0 else F32, name=f"e_{h}")
+                nc.scalar.activation(
+                    e[h, jb][:], negated[:], EXP, bias=shift[:], scale=-1.0, accum_out=total[h][:, jb : jb + 1]
+                )
 
+        x_t = [held.tile([P, NODES], BF16, name=f"x_t_{h}") for h in range(HEADS)]
+
+        def flip_x(h, copy):
+            x_t_bank = score_banks.tile([P, NODES], BF16, name="x_t_bank", tag="scores")
+            for kb in range(BLOCKS):
+                nc.tensor.matmul(x_t_bank[:, block(kb)], x_bf16[h][:, block(kb)], identity[:], start=True, stop=True)
+            copy(x_t[h][:], x_t_bank[:])
+
+        flip_x(0, nc.vector.tensor_copy)
+        inverse = held.tile([P, BLOCKS], F32, name="inverse")
+        nc.vector.reciprocal(inverse[:], total[0][:])
+        inverse_high = held.tile([P, BLOCKS], BF16, name="inverse_high")
+        with nc.allow_low_precision(reason="inverse_low makes up for the rounding"):
+            nc.vector.reciprocal(inverse_high[:], total[0][:])
+        inverse_low = held.tile([P, BLOCKS], BF16, name="inverse_low")
+        nc.vector.tensor_tensor(inverse_low[:], inverse[:], inverse_high[:], SUBTRACT)
+        inverse_bank = score_banks.tile([P, NODES], F32, name="inverse_bank", tag="scores")
+        for jb in range(BLOCKS):
+            for term, first in ((inverse_high, True), (inverse_low, False)):
+                nc.tensor.matmul(
+                    inverse_bank[:, block(jb)],
+                    term[:, jb : jb + 1].to_broadcast([P, P]),
+                    identity[:],
+                    start=first,
+                    stop=not first,
+                )
+        inverse_rows = held.tile([P, NODES], F32, name="inverse_rows")
+        nc.scalar.copy(inverse_rows[:], inverse_bank[:])
+
+        e_t_bank = flipped_banks.tile([P, BLOCKS, NODES], BF16, name="e_t_bank", tag="flipped")
+        for jb in range(BLOCKS):
+            for kb in range(BLOCKS):
+                nc.tensor.matmul(
+                    e_t_bank[:, jb, block(kb)], e[0, jb][:, block(kb)], identity[:], start=True, stop=True
+                )
+        e_t = held.tile([P, BLOCKS, NODES], BF16, name="e_t")
+        nc.vector.tensor_copy(e_t[:], e_t_bank[:])
+        y = [held.tile([P, NODES], F32, name=f"y_{h}") for h in range(HEADS)]
+        for jb in range(BLOCKS):
+            weighted = sum_banks.tile([P, P], F32, name="weighted")
+            for kb in range(BLOCKS):
+                nc.tensor.matmul(
+                    weighted[:],
+                    x_t[0][:, block(kb)],
+                    e_t[:, jb, block(kb)],
+                    start=(kb == 0),
+                    stop=(kb == BLOCKS - 1),
+                )
+            nc.vector.tensor_tensor(y[0][:, block(jb)], weighted[:], inverse_rows[:, block(jb)], MULT)
+
+        flip_x(1, nc.scalar.copy)
+        for jb in range(BLOCKS):
+            inverse_1 = rows.tile([P, 1], F32, name="inverse_1")
+            nc.vector.reciprocal(inverse_1[:], total[1][:, jb : jb + 1])
+            weights = rows.tile([P, NODES], BF16, name="weights")
+            nc.vector.tensor_scalar_mul(weights[:], e[1, jb][:], inverse_1[:])
+            weights_t_bank = flipped_banks.tile([P, NODES], BF16, name="flipped")
+            for kb in range(BLOCKS):
+                nc.tensor.matmul(
+                    weights_t_bank[:, block(kb)], weights[:, block(kb)], identity[:], start=True, stop=True
+                )
+            weights_t = rows.tile([P, NODES], BF16, name="weights_t")
+            nc.scalar.copy(weights_t[:], weights_t_bank[:])
+            weighted_1 = sum_banks.tile([P, P], F32, name="weighted_1", tag="weighted")
+            for kb in range(BLOCKS):
+                nc.tensor.matmul(
+                    weighted_1[:],
+                    x_t[1][:, block(kb)],
+                    weights_t[:, block(kb)],
+                    start=(kb == 0),
+                    stop=(kb == BLOCKS - 1),
+                )
+            nc.scalar.activation(y[1][:, block(jb)], weighted_1[:], IDENTITY, bias=bias[1][:])
+
+        residual = (x_bias, x_f32[1])
         for h in range(HEADS):
-            nc.vector.tensor_tensor(window[h][:].indirect(offsets[:]), x_f32[h][:], y[h][:], ADD)
+            nc.vector.tensor_tensor(window[h][:].indirect(offsets[:]), residual[h][:], y[h][:], ADD)
             queues[h].dma_start(out[block(h), :], window[h][:])

@@ -101,7 +101,7 @@ def tile_gat_kernel(tc, base, x, adj_t, bo, offs, out):
                     e[h, jb][:], negated[:], EXP, bias=shift[:], scale=-1.0, accum_out=total[h][:, jb : jb + 1]
                 )
 
-        x_t = [held.tile([P, NODES], BF16, name=f"x_t_{h}") for h in range(HEADS)]
+        x_t = {0: held.tile([P, NODES], BF16, name="x_t_0")}
 
         def flip_x(h, copy):
             x_t_bank = score_banks.tile([P, NODES], BF16, name="x_t_bank", tag="scores")
@@ -117,18 +117,18 @@ def tile_gat_kernel(tc, base, x, adj_t, bo, offs, out):
             nc.vector.reciprocal(inverse_high[:], total[0][:])
         inverse_low = held.tile([P, BLOCKS], BF16, name="inverse_low")
         nc.vector.tensor_tensor(inverse_low[:], inverse[:], inverse_high[:], SUBTRACT)
-        inverse_bank = score_banks.tile([P, NODES], F32, name="inverse_bank", tag="scores")
+        inverse_rows = [held.tile([P, P], F32, name=f"inverse_rows_{jb}") for jb in range(BLOCKS)]
         for jb in range(BLOCKS):
+            inverse_bank = score_banks.tile([P, P], F32, name="inverse_bank", tag="scores")
             for term, first in ((inverse_high, True), (inverse_low, False)):
                 nc.tensor.matmul(
-                    inverse_bank[:, block(jb)],
+                    inverse_bank[:],
                     term[:, jb : jb + 1].to_broadcast([P, P]),
                     identity[:],
                     start=first,
                     stop=not first,
                 )
-        inverse_rows = held.tile([P, NODES], F32, name="inverse_rows")
-        nc.scalar.copy(inverse_rows[:], inverse_bank[:])
+            nc.scalar.copy(inverse_rows[jb][:], inverse_bank[:])
 
         e_t_bank = flipped_banks.tile([P, BLOCKS, NODES], BF16, name="e_t_bank", tag="flipped")
         for jb in range(BLOCKS):
@@ -149,8 +149,9 @@ def tile_gat_kernel(tc, base, x, adj_t, bo, offs, out):
                     start=(kb == 0),
                     stop=(kb == BLOCKS - 1),
                 )
-            nc.vector.tensor_tensor(y[0][:, block(jb)], weighted[:], inverse_rows[:, block(jb)], MULT)
+            nc.vector.tensor_tensor(y[0][:, block(jb)], weighted[:], inverse_rows[jb][:], MULT)
 
+        x_t[1] = held.tile([P, NODES], BF16, name="x_t_1", tag="e_t")
         flip_x(1, nc.scalar.copy)
         for jb in range(BLOCKS):
             inverse_1 = rows.tile([P, 1], F32, name="inverse_1")

@@ -112,15 +112,13 @@ def tile_gat_kernel(tc, base, x, adj_t, bo, offs, out):
         flip_x(0, nc.vector.tensor_copy)
         inverse = held.tile([P, BLOCKS], F32, name="inverse")
         nc.vector.reciprocal(inverse[:], total[0][:])
-        inverse_high = held.tile([P, BLOCKS], BF16, name="inverse_high")
-        with nc.allow_low_precision(reason="inverse_low makes up for the rounding"):
-            nc.vector.reciprocal(inverse_high[:], total[0][:])
+        inverse_high = inverse[:].bitcast(BF16)[:, 1::2]
         inverse_low = held.tile([P, BLOCKS], BF16, name="inverse_low")
-        nc.vector.tensor_tensor(inverse_low[:], inverse[:], inverse_high[:], SUBTRACT)
+        nc.vector.tensor_tensor(inverse_low[:], inverse[:], inverse_high, SUBTRACT)
         inverse_rows = [held.tile([P, P], F32, name=f"inverse_rows_{jb}") for jb in range(BLOCKS)]
         for jb in range(BLOCKS):
             inverse_bank = score_banks.tile([P, P], F32, name="inverse_bank", tag="scores")
-            for term, first in ((inverse_high, True), (inverse_low, False)):
+            for term, first in ((inverse_high, True), (inverse_low[:], False)):
                 nc.tensor.matmul(
                     inverse_bank[:],
                     term[:, jb : jb + 1].to_broadcast([P, P]),
@@ -130,14 +128,12 @@ def tile_gat_kernel(tc, base, x, adj_t, bo, offs, out):
                 )
             nc.scalar.copy(inverse_rows[jb][:], inverse_bank[:])
 
-        e_t_bank = flipped_banks.tile([P, BLOCKS, NODES], BF16, name="e_t_bank", tag="flipped")
+        e_t = [held.tile([P, NODES], BF16, name=f"e_t_{jb}", tag=("total_0", "e_t_1")[jb]) for jb in range(BLOCKS)]
         for jb in range(BLOCKS):
+            e_t_bank = flipped_banks.tile([P, NODES], BF16, name="e_t_bank", tag="flipped")
             for kb in range(BLOCKS):
-                nc.tensor.matmul(
-                    e_t_bank[:, jb, block(kb)], e[0, jb][:, block(kb)], identity[:], start=True, stop=True
-                )
-        e_t = held.tile([P, BLOCKS, NODES], BF16, name="e_t")
-        nc.vector.tensor_copy(e_t[:], e_t_bank[:])
+                nc.tensor.matmul(e_t_bank[:, block(kb)], e[0, jb][:, block(kb)], identity[:], start=True, stop=True)
+            nc.vector.tensor_copy(e_t[jb][:], e_t_bank[:])
         y = [held.tile([P, NODES], F32, name=f"y_{h}") for h in range(HEADS)]
         for jb in range(BLOCKS):
             weighted = sum_banks.tile([P, P], F32, name="weighted")
@@ -145,13 +141,13 @@ def tile_gat_kernel(tc, base, x, adj_t, bo, offs, out):
                 nc.tensor.matmul(
                     weighted[:],
                     x_t[0][:, block(kb)],
-                    e_t[:, jb, block(kb)],
+                    e_t[jb][:, block(kb)],
                     start=(kb == 0),
                     stop=(kb == BLOCKS - 1),
                 )
             nc.vector.tensor_tensor(y[0][:, block(jb)], weighted[:], inverse_rows[jb][:], MULT)
 
-        x_t[1] = held.tile([P, NODES], BF16, name="x_t_1", tag="e_t")
+        x_t[1] = held.tile([P, NODES], BF16, name="x_t_1", tag="e_t_1")
         flip_x(1, nc.scalar.copy)
         for jb in range(BLOCKS):
             inverse_1 = rows.tile([P, 1], F32, name="inverse_1")

import math

import concourse.mybir as mybir
from concourse.masks import make_identity

F32 = mybir.dt.float32
BF16 = mybir.dt.bfloat16
U16 = mybir.dt.uint16
ADD = mybir.AluOpType.add
MULT = mybir.AluOpType.mult
MIN = mybir.AluOpType.min
SUBTRACT = mybir.AluOpType.subtract
EXP = mybir.ActivationFunctionType.Exp
IDENTITY = mybir.ActivationFunctionType.Identity

P = 128
HEADS = 2
NODES = 256
SLOTS = 512
BLOCKS = NODES // P
SCALE = 1.0 / math.sqrt(P)
NO_EDGE = -32768.0

WARMING_ROWS = 32
WARMING_MATMULS = 14

FLOPS = 4 * HEADS * P * NODES * NODES


def block(i):
    return slice(i * P, (i + 1) * P)


def tile_gat_kernel(tc, base, x, adj_t, bo, offs, out):
    nc = tc.nc
    with (
        tc.tile_pool(name="held", bufs=1) as held,
        tc.tile_pool(name="rows", bufs=HEADS * BLOCKS) as rows,
        tc.psum_pool(name="score_banks", bufs=HEADS * BLOCKS) as score_banks,
        tc.psum_pool(name="flipped_banks", bufs=2) as flipped_banks,
        tc.psum_pool(name="sum_banks", bufs=HEADS) as sum_banks,
    ):
        zeros = held.tile([P, WARMING_ROWS], BF16, name="zeros")
        nc.vector.memset(zeros[:], 0.0)

        queues = (nc.sync, nc.scalar)
        x_f32 = [held.tile([P, NODES], F32, name=f"x_f32_{h}") for h in range(HEADS)]
        adj = [held.tile([P, BLOCKS, P], F32, name=f"adj_{jb}") for jb in range(BLOCKS)]
        window = [held.tile([P, SLOTS], F32, name=f"window_{h}") for h in range(HEADS)]
        bias = [held.tile([P, 1], F32, name=f"bias_{h}") for h in range(HEADS)]
        offsets = held.tile([P, NODES // 16], U16, name="offsets")
        nc.sync.dma_start(adj[0][:], adj_t[:, block(0)].rearrange("(kb p) j -> p kb j", p=P))
        nc.scalar.dma_start(x_f32[0][:], x[block(0), :])
        nc.sync.dma_start(adj[1][:], adj_t[:, block(1)].rearrange("(kb p) j -> p kb j", p=P))
        nc.scalar.dma_start(x_f32[1][:], x[block(1), :])
        for h in range(HEADS):
            queues[h].dma_start(bias[h][:], bo[block(h), :])
        nc.sync.dma_start(offsets[:], offs)
        for h in range(HEADS):
            queues[h].dma_start(window[h][:], base[block(h), :])

        warm = held.tile([P, 1], F32, name="warm")
        nc.scalar.activation(warm[:], zeros[:, 0:1], EXP)

        identity = held.tile([P, P], BF16, name="identity")
        make_identity(nc, identity[:])

        idle_bank = score_banks.tile([P, P], F32, name="scores")
        for i in range(WARMING_MATMULS):
            nc.tensor.matmul(
                idle_bank[:WARMING_ROWS, :], zeros[:], zeros[:, 0:1].to_broadcast([P, P]), start=True, stop=True
            )

        x_bf16 = [held.tile([P, NODES], BF16, name=f"x_bf16_{h}") for h in range(HEADS)]
        no_edge = [held.tile([P, BLOCKS, P], BF16, name=f"no_edge_{jb}") for jb in range(BLOCKS)]
        for i in range(HEADS):
            nc.vector.tensor_scalar(no_edge[i][:], adj[i][:], -NO_EDGE, NO_EDGE, MULT, ADD)
            nc.vector.tensor_copy(x_bf16[i][:], x_f32[i][:])

        scores = {}
        for h in range(HEADS):
            for jb in range(BLOCKS):
                scores[h, jb] = score_banks.tile([P, NODES], F32, name="scores")
                for kb in range(BLOCKS):
                    nc.tensor.matmul(
                        scores[h, jb][:, block(kb)], no_edge[jb][:, kb, :], identity[:], start=(kb == 0), stop=False
                    )
                nc.tensor.matmul(scores[h, jb][:], x_bf16[h][:, block(jb)], x_bf16[h][:], start=False, stop=True)

        x_bias = held.tile([P, NODES], F32, name="x_bias")
        nc.scalar.activation(x_bias[:], x_f32[0][:], IDENTITY, bias=bias[0][:])
        e, total = {}, {}
        for h in range(HEADS):
            total[h] = held.tile([P, BLOCKS], F32, name=f"total_{h}")
            for jb in range(BLOCKS):
                negated = rows.tile([P, NODES], F32, name="negated")
                shift = rows.tile([P, 1], F32, name="shift")
                nc.vector.tensor_scalar(negated[:], scores[h, jb][:], -SCALE, None, MULT, MIN, accum_out=shift[:])
                e[h, jb] = rows.tile([P, NODES], BF16 if h == 0 else F32, name=f"e_{h}")
                nc.scalar.activation(
                    e[h, jb][:], negated[:], EXP, bias=shift[:], scale=-1.0, accum_out=total[h][:, jb : jb + 1]
                )

        x_t = {0: held.tile([P, NODES], BF16, name="x_t_0")}

        def flip_x(h, copy):
            x_t_bank = score_banks.tile([P, NODES], BF16, name="x_t_bank", tag="scores")
            for kb in range(BLOCKS):
                nc.tensor.matmul(x_t_bank[:, block(kb)], x_bf16[h][:, block(kb)], identity[:], start=True, stop=True)
            copy(x_t[h][:], x_t_bank[:])

        flip_x(0, nc.vector.tensor_copy)
        inverse = held.tile([P, BLOCKS], F32, name="inverse")
        nc.vector.reciprocal(inverse[:], total[0][:])
        inverse_high = inverse[:].bitcast(BF16)[:, 1::2]
        inverse_low = held.tile([P, BLOCKS], BF16, name="inverse_low")
        nc.vector.tensor_tensor(inverse_low[:], inverse[:], inverse_high, SUBTRACT)
        inverse_rows = [held.tile([P, P], F32, name=f"inverse_rows_{jb}") for jb in range(BLOCKS)]
        for jb in range(BLOCKS):
            inverse_bank = score_banks.tile([P, P], F32, name="inverse_bank", tag="scores")
            for term, first in ((inverse_high, True), (inverse_low[:], False)):
                nc.tensor.matmul(
                    inverse_bank[:],
                    term[:, jb : jb + 1].to_broadcast([P, P]),
                    identity[:],
                    start=first,
                    stop=not first,
                )
            nc.scalar.copy(inverse_rows[jb][:], inverse_bank[:])

        e_t = [held.tile([P, NODES], BF16, name=f"e_t_{jb}", tag=("total_0", "e_t_1")[jb]) for jb in range(BLOCKS)]
        for jb in range(BLOCKS):
            e_t_bank = flipped_banks.tile([P, NODES], BF16, name="e_t_bank", tag="flipped")
            for kb in range(BLOCKS):
                nc.tensor.matmul(e_t_bank[:, block(kb)], e[0, jb][:, block(kb)], identity[:], start=True, stop=True)
            nc.vector.tensor_copy(e_t[jb][:], e_t_bank[:])
        y = [held.tile([P, NODES], F32, name=f"y_{h}") for h in range(HEADS)]
        for jb in range(BLOCKS):
            weighted = sum_banks.tile([P, P], F32, name="weighted")
            for kb in range(BLOCKS):
                nc.tensor.matmul(
                    weighted[:],
                    x_t[0][:, block(kb)],
                    e_t[jb][:, block(kb)],
                    start=(kb == 0),
                    stop=(kb == BLOCKS - 1),
                )
            nc.vector.tensor_tensor(y[0][:, block(jb)], weighted[:], inverse_rows[jb][:], MULT)

        x_t[1] = held.tile([P, NODES], BF16, name="x_t_1", tag="e_t_1")
        flip_x(1, nc.scalar.copy)
        for jb in range(BLOCKS):
            inverse_1 = rows.tile([P, 1], F32, name="inverse_1")
            nc.vector.reciprocal(inverse_1[:], total[1][:, jb : jb + 1])
            weights = rows.tile([P, NODES], BF16, name="weights")
            nc.vector.tensor_scalar_mul(weights[:], e[1, jb][:], inverse_1[:])
            weights_t_bank = flipped_banks.tile([P, NODES], BF16, name="flipped")
            for kb in range(BLOCKS):
                nc.tensor.matmul(
                    weights_t_bank[:, block(kb)], weights[:, block(kb)], identity[:], start=True, stop=True
                )
            weights_t = rows.tile([P, NODES], BF16, name="weights_t")
            nc.scalar.copy(weights_t[:], weights_t_bank[:])
            weighted_1 = sum_banks.tile([P, P], F32, name="weighted_1", tag="weighted")
            for kb in range(BLOCKS):
                nc.tensor.matmul(
                    weighted_1[:],
                    x_t[1][:, block(kb)],
                    weights_t[:, block(kb)],
                    start=(kb == 0),
                    stop=(kb == BLOCKS - 1),
                )
            nc.scalar.activation(y[1][:, block(jb)], weighted_1[:], IDENTITY, bias=bias[1][:])

        residual = (x_bias, x_f32[1])
        for h in range(HEADS):
            nc.vector.tensor_tensor(window[h][:].indirect(offsets[:]), residual[h][:], y[h][:], ADD)
            queues[h].dma_start(out[block(h), :], window[h][:])
